import numpy as np
import ml_dtypes


def mxq(x, axis, fmt="e4m3"):
    dtype, down = {"e4m3": (ml_dtypes.float8_e4m3fn, 7), "e5m2": (ml_dtypes.float8_e5m2, 14)}[fmt]
    v = np.moveaxis(np.asarray(x, np.float32).astype(ml_dtypes.bfloat16).astype(np.float64), axis, -1)
    blocks = v.reshape(v.shape[:-1] + (-1, 32))
    amax = np.abs(blocks).max(-1, keepdims=True)
    byte = np.maximum(np.where(amax > 0, np.frexp(amax)[1] - 1 + 127, 0) - down, 1)
    scale = np.exp2(byte - 127.0)
    codes = (blocks / scale).astype(np.float32).astype(dtype).astype(np.float64)
    return np.moveaxis((codes * scale).reshape(v.shape), -1, axis)


WIDE = False


def mx_kscale(k):
    if not WIDE:
        return np.ones(k)
    levels = np.array([10, -10, 5, -5, 0])
    a = np.random.permutation(np.resize(levels, k // 512 * 4)).reshape(k // 512, 4)
    idx = np.arange(k)
    return np.exp2(a[idx // 512, idx % 128 // 32])


BF16 = ml_dtypes.bfloat16


def bf(x):
    return np.asarray(x, np.float32).astype(BF16)


def f64(x):
    return np.asarray(x).astype(np.float64)


B, H, W, C, NH, WS, SHIFT, F = 4, 32, 32, 512, 16, 8, 3, 4096
S = WS * WS
HD = C // NH
EPS = 1e-5


def layer_norm(x, w, b):
    m = x.mean(-1, keepdims=True)
    v = ((x - m) ** 2).mean(-1, keepdims=True)
    return (x - m) / np.sqrt(v + EPS) * w + b


def to_heads(t):
    return t.reshape(-1, S, NH, HD).transpose(0, 2, 1, 3)


def setup_inputs():
    s = mx_kscale(C)
    return {"x": bf(np.random.standard_normal((B, H * W, C))),
            "norm1_w": bf((1.0 + 0.1 * np.random.standard_normal(C)) * s),
            "norm1_b": bf(0.1 * np.random.standard_normal(C) * s),
            "qkv_w": bf(np.random.standard_normal((3 * C, C)) / np.sqrt(C) / s[None, :]),
            "qkv_b": bf(0.1 * np.random.standard_normal(3 * C))}


def reference(x, norm1_w, norm1_b, qkv_w, qkv_b):
    h = layer_norm(f64(x), f64(norm1_w), f64(norm1_b)).reshape(B, H, W, C)
    h = np.roll(h, (-SHIFT, -SHIFT), axis=(1, 2))
    win = h.reshape(B, H // WS, WS, W // WS, WS, C)
    win = win.transpose(0, 1, 3, 2, 4, 5).reshape(-1, S, C)
    win = win
    qkv = (mxq(win, 2, "e4m3") @ mxq(f64(qkv_w), 1, "e4m3").T) + f64(qkv_b)
    q, k, v = np.split(qkv, 3, axis=-1)
    return to_heads(q), to_heads(k), to_heads(v)

@@ -1,0 +1,301 @@
+from contextlib import ExitStack
+
+import concourse.mybir as mybir
+from concourse.masks import make_identity
+
+F32 = mybir.dt.float32
+BF16 = mybir.dt.bfloat16
+U32 = mybir.dt.uint32
+U8 = mybir.dt.uint8
+FP8X4 = mybir.dt.float8_e4m3fn_x4
+ACT = mybir.ActivationFunctionType
+ALU = mybir.AluOpType
+
+P = 128
+PACK = 4
+BANK = 512
+IMAGES, SIDE, CHANNELS = 4, 32, 512
+WINDOW = 8
+BLOCKS = SIDE // WINDOW
+SHIFT = 3
+HEADS, HEAD_DIM = 16, 32
+EPS = 1e-5
+TOKENS = IMAGES * SIDE * SIDE
+OUT_CHANNELS = 3 * CHANNELS
+FLOPS = 2 * TOKENS * CHANNELS * OUT_CHANNELS
+
+ROWS_LOW = 4
+ROUND = 4
+WEIGHT_TILES = OUT_CHANNELS // P
+
+CHUNK = 256
+CHUNKS = OUT_CHANNELS // CHUNK
+HEADS_PER_CHUNK = CHUNK // HEAD_DIM
+CHUNKS_PER_OUTPUT = CHANNELS // CHUNK
+TILES_PER_BANK = BANK // CHUNK
+
+ROWS_PER_GROUP = 1
+GROUPS = ROWS_LOW // ROWS_PER_GROUP
+PLACES = ROWS_PER_GROUP * WINDOW
+ROUNDS_PER_GROUP = PLACES // ROUND
+ROUNDS = GROUPS * ROUNDS_PER_GROUP
+LN_STAGES = CHUNKS // ROUNDS_PER_GROUP
+BANKS_PER_CHUNK = PLACES // TILES_PER_BANK
+
+SHARE = 8
+VECTOR_SHARE = 4
+
+
+def rotate_columns(nc, out, in_, block, shift):
+    dst = out.rearrange("p (g c) -> p g c", c=block)
+    src = in_.rearrange("p (g c) -> p g c", c=block)
+    nc.vector.tensor_copy(out=dst[:, :, 0 : block - shift], in_=src[:, :, shift:block])
+    nc.vector.tensor_copy(out=dst[:, :, block - shift : block], in_=src[:, :, 0:shift])
+
+
+def tile_swintransformerblock_pa_t_kernel(
+    tc, x, norm1_w, norm1_b, qkv_w, qkv_b, out_0, out_1, out_2
+):
+    nc = tc.nc
+    outs = (out_0, out_1, out_2)
+
+    with ExitStack() as ctx:
+        const = ctx.enter_context(tc.tile_pool(name="const", bufs=1))
+        small = ctx.enter_context(tc.tile_pool(name="small", bufs=4))
+        z_pool = ctx.enter_context(tc.tile_pool(name="z", bufs=3))
+        stage = ctx.enter_context(tc.tile_pool(name="stage", bufs=2))
+        o_pool = ctx.enter_context(tc.tile_pool(name="o", bufs=CHUNKS))
+        turned = ctx.enter_context(tc.psum_pool(name="turned", bufs=4))
+        products = ctx.enter_context(tc.psum_pool(name="products", bufs=4))
+        ctx.enter_context(tc.manual_schedule())
+
+        x_view = x.rearrange(
+            "b (iq il jb jc) k -> il jb (b iq) jc k", il=ROWS_LOW, jb=BLOCKS, jc=WINDOW
+        )
+        x_tiles = [
+            const.tile([P, WINDOW, CHANNELS], BF16, name="x_il%d" % il) for il in range(ROWS_LOW)
+        ]
+
+        def load_x(r_lo):
+            il = (r_lo + SHIFT) % ROWS_LOW
+            for jb in range(BLOCKS):
+                nc.sync.dma_start(out=x_tiles[il][jb:P:BLOCKS, :, :], in_=x_view[il, jb])
+
+        gain_bias_rows = const.tile([P, P], BF16)
+        nc.vector.memset(gain_bias_rows[:], 0.0)
+        nc.scalar.dma_start(
+            out=gain_bias_rows[0:PACK, :], in_=norm1_w.rearrange("(t p) -> t p", p=P)
+        )
+        nc.scalar.dma_start(
+            out=gain_bias_rows[PACK : 2 * PACK, :], in_=norm1_b.rearrange("(t p) -> t p", p=P)
+        )
+
+        w_raw = const.tile([P, WEIGHT_TILES, CHANNELS], BF16)
+        qkv_bias_bf = const.tile([P, OUT_CHANNELS], BF16)
+        load_x(0)
+        load_x(1)
+        nc.sync.dma_start(out=w_raw[:], in_=qkv_w.rearrange("(f p) k -> p f k", p=P))
+        nc.sync.dma_start(out=qkv_bias_bf[:], in_=qkv_b.partition_broadcast(P))
+        load_x(2)
+        load_x(3)
+
+        ident_bf = const.tile([P, P], BF16)
+        make_identity(nc, ident_bf[:])
+        ident = const.tile([P, P], F32)
+        make_identity(nc, ident[:])
+        eps_col = const.tile([P, 1], F32)
+        nc.vector.memset(eps_col[:], EPS)
+
+        rolled = {(0, 0): ident}
+        for rs, cs in ((0, 1), (1, 0), (1, 1)):
+            rolled[(rs, cs)] = const.tile([P, P], F32, name="rolled%d%d" % (rs, cs))
+        rotate_columns(nc, rolled[(0, 1)][:], ident[:], block=4, shift=1)
+        rotate_columns(nc, rolled[(1, 0)][:], ident[:], block=32, shift=4)
+        rotate_columns(nc, rolled[(1, 1)][:], rolled[(0, 1)][:], block=32, shift=4)
+        perm = {}
+        for key in rolled:
+            perm[key] = const.tile([P, P], F32, name="perm%d%d" % key)
+            nc.vector.tensor_copy(
+                out=perm[key][:].rearrange("p (m wj rh) -> p m rh wj", wj=4, rh=2),
+                in_=rolled[key][:].rearrange("p (m rh wj) -> p m rh wj", rh=2, wj=4),
+            )
+
+        gain_bias_t = turned.tile([P, P], BF16, tag="turned")
+        nc.tensor.transpose(out=gain_bias_t[:], in_=gain_bias_rows[:], identity=ident_bf[:])
+        gain_bias = const.tile([P, 2 * PACK], F32)
+        nc.vector.tensor_copy(out=gain_bias[:], in_=gain_bias_t[:, 0 : 2 * PACK])
+
+        qkv_bias = const.tile([P, OUT_CHANNELS], F32)
+
+        x_codes = const.tile([P, TOKENS], U32, align_bytes=64)
+        x_scales = const.tile([P, TOKENS], U8, align_bytes=64)
+        w_codes = const.tile([P, OUT_CHANNELS], U32, align_bytes=64)
+        w_scales = const.tile([P, OUT_CHANNELS], U8, align_bytes=64)
+
+        mean_var_of, std_of, z_of, turned_of, planes_of = {}, {}, {}, {}, {}
+
+        def source(i, u):
+            r_lo, c = divmod(ROUND * i + u, WINDOW)
+            key = (1 if r_lo > 0 else 0, 1 if c + SHIFT >= WINDOW else 0)
+            return x_tiles[(r_lo + SHIFT) % ROWS_LOW][:, (c + SHIFT) % WINDOW, :], perm[key]
+
+        def measure(i):
+            stats = small.tile([P, ROUND, 6], F32)
+            mean_var_of[i] = small.tile([P, ROUND, 2], F32, name="mean_var")
+            for u in range(ROUND):
+                nc.vector.bn_stats(out=stats[:, u, :], in_=source(i, u)[0])
+            for u in range(ROUND):
+                nc.vector.bn_aggr(out=mean_var_of[i][:, u, :], in_=stats[:, u, :])
+
+        def measure_scalar(i):
+            std_of[i] = small.tile([P, ROUND], F32, name="std")
+            nc.scalar.activation(
+                out=std_of[i][:], in_=mean_var_of[i][:, :, 1], func=ACT.Sqrt, bias=eps_col[:],
+                scale=1.0,
+            )
+
+        def centre(i):
+            rstd = small.tile([P, ROUND], F32)
+            nc.vector.reciprocal(out=rstd[:], in_=std_of[i][:])
+            z_of[i] = z_pool.tile([P, ROUND, CHANNELS], F32, name="z")
+            for u in range(ROUND):
+                nc.vector.tensor_scalar(
+                    out=z_of[i][:, u, :], in0=source(i, u)[0],
+                    scalar1=mean_var_of[i][:, u, 0:1], scalar2=rstd[:, u : u + 1],
+                    op0=ALU.subtract, op1=ALU.mult,
+                )
+
+        def turn(i):
+            turned_of[i] = []
+            for t in range(PACK):
+                z_t = turned.tile([P, ROUND, P], F32, tag="turned")
+                for u in range(ROUND):
+                    nc.tensor.transpose(
+                        out=z_t[:, u, :], in_=z_of[i][:, u, P * t : P * (t + 1)],
+                        identity=source(i, u)[1][:],
+                    )
+                turned_of[i].append(z_t)
+
+        def centre_and_turn(i):
+            centre(i)
+            turn(i)
+
+        def scale_out(i):
+            planes_of[i] = stage.tile([P, PACK, ROUND * P], BF16, name="h_planes")
+            for t in range(PACK):
+                nc.scalar.activation(
+                    out=planes_of[i][:, t, :], in_=turned_of[i][t][:].rearrange("p u r -> p (u r)"),
+                    func=ACT.Identity,
+                    scale=gain_bias[:, t : t + 1], bias=gain_bias[:, PACK + t : PACK + t + 1],
+                )
+
+        def pack(i):
+            h_words = stage.tile([P, ROUND * P, PACK], BF16, align_bytes=64)
+            nc.vector.tensor_copy(out=h_words[:], in_=planes_of[i][:].rearrange("p t r -> p r t"))
+            columns = slice(ROUND * P * i, ROUND * P * (i + 1))
+            nc.vector.quantize_mx(
+                out=x_codes[:, columns].bitcast(FP8X4),
+                scales=x_scales[:, columns],
+                in_=h_words[:].rearrange("p r t -> p (r t)"),
+            )
+
+        def quantise_weights(chunk):
+            tiles = CHUNK // P
+            w_t = turned.tile([P, tiles, PACK, P], BF16, tag="turned")
+            for f in range(tiles):
+                for t in range(PACK):
+                    nc.tensor.transpose(
+                        out=w_t[:, f, t, :], in_=w_raw[:, tiles * chunk + f, P * t : P * (t + 1)],
+                        identity=ident_bf[:],
+                    )
+            w_words = stage.tile([P, tiles, P, PACK], BF16, align_bytes=64)
+            nc.scalar.copy(out=w_words[:], in_=w_t[:].rearrange("p f t c -> p f c t"))
+            nc.vector.quantize_mx(
+                out=w_codes[:, CHUNK * chunk : CHUNK * (chunk + 1)].bitcast(FP8X4),
+                scales=w_scales[:, CHUNK * chunk : CHUNK * (chunk + 1)],
+                in_=w_words[:].rearrange("p f c t -> p (f c t)"),
+            )
+
+        def multiply(group, chunk):
+            channels = slice(CHUNK * chunk, CHUNK * (chunk + 1))
+            banks = []
+            for bank in range(BANKS_PER_CHUNK):
+                acc = products.tile([P, TILES_PER_BANK, CHUNK], F32)
+                for u in range(TILES_PER_BANK):
+                    first = P * (PLACES * group + TILES_PER_BANK * bank + u)
+                    nc.tensor.matmul_mx(
+                        out=acc[:, u, :],
+                        lhsT=x_codes[:, first : first + P].bitcast(FP8X4),
+                        lhsT_scale=x_scales[:, first : first + P],
+                        rhs=w_codes[:, channels].bitcast(FP8X4),
+                        rhs_scale=w_scales[:, channels],
+                        start=True,
+                        stop=True,
+                    )
+                banks.append(acc)
+            return banks
+
+        def store(group, chunk, banks):
+            bias = (
+                qkv_bias[:, CHUNK * chunk : CHUNK * (chunk + 1)]
+                .rearrange("p (a d) -> p a d", d=HEAD_DIM)
+                .unsqueeze(1)
+                .to_broadcast([P, TILES_PER_BANK, HEADS_PER_CHUNK, HEAD_DIM])
+            )
+            o_tile = o_pool.tile([P, HEADS_PER_CHUNK, PLACES, HEAD_DIM], F32)
+            for bank, acc in enumerate(banks):
+                dst = o_tile[
+                    :, :, TILES_PER_BANK * bank : TILES_PER_BANK * (bank + 1), :
+                ].rearrange("p a s d -> p s a d")
+                src = acc[:].rearrange("p s (a d) -> p s a d", d=HEAD_DIM)
+                number = BANKS_PER_CHUNK * (CHUNKS * group + chunk) + bank
+                if number * VECTOR_SHARE % SHARE < VECTOR_SHARE:
+                    nc.vector.tensor_tensor(out=dst, in0=src, in1=bias, op=ALU.add)
+                else:
+                    nc.scalar.copy(out=dst, in_=src)
+                    nc.gpsimd.tensor_tensor(out=dst, in0=dst, in1=bias, op=ALU.add)
+            out = outs[chunk // CHUNKS_PER_OUTPUT]
+            head = HEADS_PER_CHUNK * (chunk % CHUNKS_PER_OUTPUT)
+            for rh in range(2):
+                place = ROWS_LOW * WINDOW * rh + PLACES * group
+                nc.sync.dma_start(
+                    out=out[:, head : head + HEADS_PER_CHUNK, place : place + PLACES, :],
+                    in_=o_tile[rh:P:2, :, :, :],
+                )
+
+        measure(0)
+        measure_scalar(0)
+        measure(1)
+        measure_scalar(1)
+        centre_and_turn(0)
+        scale_out(0)
+        centre_and_turn(1)
+        scale_out(1)
+        measure(2)
+        measure_scalar(2)
+        pack(0)
+        nc.vector.tensor_copy(out=qkv_bias[:], in_=qkv_bias_bf[:])
+        quantise_weights(0)
+        pack(1)
+        for chunk in range(1, CHUNKS):
+            quantise_weights(chunk)
+        centre_and_turn(2)
+        scale_out(2)
+
+        for step in range(GROUPS * CHUNKS):
+            group, chunk = divmod(step, CHUNKS)
+            i, ln_stage = 3 + step // LN_STAGES, step % LN_STAGES
+            banks = multiply(group, chunk)
+            if ln_stage == 0 and i < ROUNDS:
+                measure(i)
+            if ln_stage == 1 and i < ROUNDS:
+                centre(i)
+            if ln_stage == 2 and i < ROUNDS:
+                turn(i)
+            if ln_stage == 2 and i - 1 < ROUNDS:
+                pack(i - 1)
+            store(group, chunk, banks)
+            if ln_stage == 0 and i < ROUNDS:
+                measure_scalar(i)
+            if ln_stage == 2 and i < ROUNDS:
+                scale_out(i)

@@ -33,6 +33,7 @@ CHUNKS = OUT_CHANNELS // CHUNK
 HEADS_PER_CHUNK = CHUNK // HEAD_DIM
 CHUNKS_PER_OUTPUT = CHANNELS // CHUNK
 TILES_PER_BANK = BANK // CHUNK
+HEADS_PER_STORE = 4
 
 ROWS_PER_GROUP = 1
 GROUPS = ROWS_LOW // ROWS_PER_GROUP
@@ -258,10 +259,13 @@ def tile_swintransformerblock_pa_t_kernel(
             head = HEADS_PER_CHUNK * (chunk % CHUNKS_PER_OUTPUT)
             for rh in range(2):
                 place = ROWS_LOW * WINDOW * rh + PLACES * group
-                nc.sync.dma_start(
-                    out=out[:, head : head + HEADS_PER_CHUNK, place : place + PLACES, :],
-                    in_=o_tile[rh:P:2, :, :, :],
-                )
+                for a in range(0, HEADS_PER_CHUNK, HEADS_PER_STORE):
+                    nc.sync.dma_start(
+                        out=out[
+                            :, head + a : head + a + HEADS_PER_STORE, place : place + PLACES, :
+                        ],
+                        in_=o_tile[rh:P:2, a : a + HEADS_PER_STORE, :, :],
+                    )
 
         measure(0)
         measure_scalar(0)

@@ -24,8 +24,10 @@ TOKENS = IMAGES * SIDE * SIDE
 OUT_CHANNELS = 3 * CHANNELS
 FLOPS = 2 * TOKENS * CHANNELS * OUT_CHANNELS
 
-ROWS_LOW = 4
+GROUPS = 4
 ROUND = 4
+ROUNDS = GROUPS * WINDOW // ROUND
+FIRST_HALF, SECOND_HALF = (0, 1), (2, 3)
 WEIGHT_TILES = OUT_CHANNELS // P
 
 CHUNK = 256
@@ -33,18 +35,8 @@ CHUNKS = OUT_CHANNELS // CHUNK
 HEADS_PER_CHUNK = CHUNK // HEAD_DIM
 CHUNKS_PER_OUTPUT = CHANNELS // CHUNK
 TILES_PER_BANK = BANK // CHUNK
-HEADS_PER_STORE = 4
-
-ROWS_PER_GROUP = 1
-GROUPS = ROWS_LOW // ROWS_PER_GROUP
-PLACES = ROWS_PER_GROUP * WINDOW
-ROUNDS_PER_GROUP = PLACES // ROUND
-ROUNDS = GROUPS * ROUNDS_PER_GROUP
-LN_STAGES = CHUNKS // ROUNDS_PER_GROUP
-BANKS_PER_CHUNK = PLACES // TILES_PER_BANK
-
-SHARE = 8
-VECTOR_SHARE = 4
+BANKS_PER_CHUNK = WINDOW // TILES_PER_BANK
+PERIOD = CHUNKS * ROUND // WINDOW
 
 
 def rotate_columns(nc, out, in_, block, shift):
@@ -71,16 +63,19 @@ def tile_swintransformerblock_pa_t_kernel(
         ctx.enter_context(tc.manual_schedule())
 
         x_view = x.rearrange(
-            "b (iq il jb jc) k -> il jb (b iq) jc k", il=ROWS_LOW, jb=BLOCKS, jc=WINDOW
+            "b (iq il jb jc) k -> il jb (b iq) jc k", il=GROUPS, jb=BLOCKS, jc=WINDOW
         )
         x_tiles = [
-            const.tile([P, WINDOW, CHANNELS], BF16, name="x_il%d" % il) for il in range(ROWS_LOW)
+            const.tile([P, WINDOW, CHANNELS], BF16, name="x_il%d" % il) for il in range(GROUPS)
         ]
 
-        def load_x(r_lo):
-            il = (r_lo + SHIFT) % ROWS_LOW
+        def load_round(i):
+            il = (i * ROUND // WINDOW + SHIFT) % GROUPS
+            columns = slice(i * ROUND % WINDOW, i * ROUND % WINDOW + ROUND)
             for jb in range(BLOCKS):
-                nc.sync.dma_start(out=x_tiles[il][jb:P:BLOCKS, :, :], in_=x_view[il, jb])
+                nc.sync.dma_start(
+                    out=x_tiles[il][jb:P:BLOCKS, columns, :], in_=x_view[il, jb][:, columns, :]
+                )
 
         gain_bias_rows = const.tile([P, P], BF16)
         nc.vector.memset(gain_bias_rows[:], 0.0)
@@ -93,12 +88,12 @@ def tile_swintransformerblock_pa_t_kernel(
 
         w_raw = const.tile([P, WEIGHT_TILES, CHANNELS], BF16)
         qkv_bias_bf = const.tile([P, OUT_CHANNELS], BF16)
-        load_x(0)
-        load_x(1)
+        for i in range(4):
+            load_round(i)
         nc.sync.dma_start(out=w_raw[:], in_=qkv_w.rearrange("(f p) k -> p f k", p=P))
         nc.sync.dma_start(out=qkv_bias_bf[:], in_=qkv_b.partition_broadcast(P))
-        load_x(2)
-        load_x(3)
+        for i in range(4, ROUNDS):
+            load_round(i)
 
         ident_bf = const.tile([P, P], BF16)
         make_identity(nc, ident_bf[:])
@@ -133,37 +128,48 @@ def tile_swintransformerblock_pa_t_kernel(
         w_codes = const.tile([P, OUT_CHANNELS], U32, align_bytes=64)
         w_scales = const.tile([P, OUT_CHANNELS], U8, align_bytes=64)
 
-        mean_var_of, std_of, z_of, turned_of, planes_of = {}, {}, {}, {}, {}
+        stats_of, mean_var_of, std_of, rstd_of, offset_of = {}, {}, {}, {}, {}
+        z_of, turned_of, planes_of, words_of = {}, {}, {}, {}
 
         def source(i, u):
-            r_lo, c = divmod(ROUND * i + u, WINDOW)
-            key = (1 if r_lo > 0 else 0, 1 if c + SHIFT >= WINDOW else 0)
-            return x_tiles[(r_lo + SHIFT) % ROWS_LOW][:, (c + SHIFT) % WINDOW, :], perm[key]
+            r_lo, jc = divmod(ROUND * i + u, WINDOW)
+            key = (1 if r_lo > 0 else 0, 1 if jc < SHIFT else 0)
+            return x_tiles[(r_lo + SHIFT) % GROUPS][:, jc, :], perm[key]
 
-        def measure(i):
-            stats = small.tile([P, ROUND, 6], F32)
+        def measure(i, tiles):
+            if i not in stats_of:
+                stats_of[i] = small.tile([P, ROUND, 6], F32, name="stats")
+            for u in tiles:
+                nc.vector.bn_stats(out=stats_of[i][:, u, :], in_=source(i, u)[0])
+
+        def aggregate(i):
             mean_var_of[i] = small.tile([P, ROUND, 2], F32, name="mean_var")
             for u in range(ROUND):
-                nc.vector.bn_stats(out=stats[:, u, :], in_=source(i, u)[0])
-            for u in range(ROUND):
-                nc.vector.bn_aggr(out=mean_var_of[i][:, u, :], in_=stats[:, u, :])
+                nc.vector.bn_aggr(out=mean_var_of[i][:, u, :], in_=stats_of[i][:, u, :])
 
-        def measure_scalar(i):
+        def root(i):
             std_of[i] = small.tile([P, ROUND], F32, name="std")
             nc.scalar.activation(
                 out=std_of[i][:], in_=mean_var_of[i][:, :, 1], func=ACT.Sqrt, bias=eps_col[:],
                 scale=1.0,
             )
 
-        def centre(i):
-            rstd = small.tile([P, ROUND], F32)
-            nc.vector.reciprocal(out=rstd[:], in_=std_of[i][:])
+        def invert(i):
+            rstd_of[i] = small.tile([P, ROUND], F32, name="rstd")
+            nc.vector.reciprocal(out=rstd_of[i][:], in_=std_of[i][:])
+            offset_of[i] = small.tile([P, ROUND], F32, name="offset")
+            nc.vector.scalar_tensor_tensor(
+                out=offset_of[i][:], in0=mean_var_of[i][:, :, 0], scalar=-1.0, in1=rstd_of[i][:],
+                op0=ALU.mult, op1=ALU.mult,
+            )
+
+        def centre(i, engine):
             z_of[i] = z_pool.tile([P, ROUND, CHANNELS], F32, name="z")
             for u in range(ROUND):
-                nc.vector.tensor_scalar(
+                engine.tensor_scalar(
                     out=z_of[i][:, u, :], in0=source(i, u)[0],
-                    scalar1=mean_var_of[i][:, u, 0:1], scalar2=rstd[:, u : u + 1],
-                    op0=ALU.subtract, op1=ALU.mult,
+                    scalar1=rstd_of[i][:, u : u + 1], scalar2=offset_of[i][:, u : u + 1],
+                    op0=ALU.mult, op1=ALU.add,
                 )
 
         def turn(i):
@@ -177,27 +183,27 @@ def tile_swintransformerblock_pa_t_kernel(
                     )
                 turned_of[i].append(z_t)
 
-        def centre_and_turn(i):
-            centre(i)
-            turn(i)
-
-        def scale_out(i):
-            planes_of[i] = stage.tile([P, PACK, ROUND * P], BF16, name="h_planes")
-            for t in range(PACK):
+        def scale_out(i, planes):
+            if i not in planes_of:
+                planes_of[i] = stage.tile([P, PACK, ROUND * P], BF16, name="h_planes")
+            for t in planes:
                 nc.scalar.activation(
-                    out=planes_of[i][:, t, :], in_=turned_of[i][t][:].rearrange("p u r -> p (u r)"),
+                    out=planes_of[i][:, t, :],
+                    in_=turned_of[i][t][:].rearrange("p u r -> p (u r)"),
                     func=ACT.Identity,
                     scale=gain_bias[:, t : t + 1], bias=gain_bias[:, PACK + t : PACK + t + 1],
                 )
 
-        def pack(i):
-            h_words = stage.tile([P, ROUND * P, PACK], BF16, align_bytes=64)
-            nc.vector.tensor_copy(out=h_words[:], in_=planes_of[i][:].rearrange("p t r -> p r t"))
+        def regroup(i, copy):
+            words_of[i] = stage.tile([P, ROUND * P, PACK], BF16, name="h_words", align_bytes=64)
+            copy(out=words_of[i][:], in_=planes_of[i][:].rearrange("p t r -> p r t"))
+
+        def quantise(i):
             columns = slice(ROUND * P * i, ROUND * P * (i + 1))
             nc.vector.quantize_mx(
                 out=x_codes[:, columns].bitcast(FP8X4),
                 scales=x_scales[:, columns],
-                in_=h_words[:].rearrange("p r t -> p (r t)"),
+                in_=words_of[i][:].rearrange("p r t -> p (r t)"),
             )
 
         def quantise_weights(chunk):
@@ -223,7 +229,8 @@ def tile_swintransformerblock_pa_t_kernel(
             for bank in range(BANKS_PER_CHUNK):
                 acc = products.tile([P, TILES_PER_BANK, CHUNK], F32)
                 for u in range(TILES_PER_BANK):
-                    first = P * (PLACES * group + TILES_PER_BANK * bank + u)
+                    c = TILES_PER_BANK * bank + u
+                    first = P * (WINDOW * group + (c + SHIFT) % WINDOW)
                     nc.tensor.matmul_mx(
                         out=acc[:, u, :],
                         lhsT=x_codes[:, first : first + P].bitcast(FP8X4),
@@ -236,21 +243,20 @@ def tile_swintransformerblock_pa_t_kernel(
                 banks.append(acc)
             return banks
 
-        def store(group, chunk, banks):
+        def store(group, chunk, banks, all_on_vector):
             bias = (
                 qkv_bias[:, CHUNK * chunk : CHUNK * (chunk + 1)]
                 .rearrange("p (a d) -> p a d", d=HEAD_DIM)
                 .unsqueeze(1)
                 .to_broadcast([P, TILES_PER_BANK, HEADS_PER_CHUNK, HEAD_DIM])
             )
-            o_tile = o_pool.tile([P, HEADS_PER_CHUNK, PLACES, HEAD_DIM], F32)
+            o_tile = o_pool.tile([P, HEADS_PER_CHUNK, WINDOW, HEAD_DIM], F32)
             for bank, acc in enumerate(banks):
                 dst = o_tile[
                     :, :, TILES_PER_BANK * bank : TILES_PER_BANK * (bank + 1), :
-                ].rearrange("p a s d -> p s a d")
-                src = acc[:].rearrange("p s (a d) -> p s a d", d=HEAD_DIM)
-                number = BANKS_PER_CHUNK * (CHUNKS * group + chunk) + bank
-                if number * VECTOR_SHARE % SHARE < VECTOR_SHARE:
+                ].rearrange("p a c d -> p c a d")
+                src = acc[:].rearrange("p c (a d) -> p c a d", d=HEAD_DIM)
+                if all_on_vector or bank % 2 == 0:
                     nc.vector.tensor_tensor(out=dst, in0=src, in1=bias, op=ALU.add)
                 else:
                     nc.scalar.copy(out=dst, in_=src)
@@ -258,48 +264,63 @@ def tile_swintransformerblock_pa_t_kernel(
             out = outs[chunk // CHUNKS_PER_OUTPUT]
             head = HEADS_PER_CHUNK * (chunk % CHUNKS_PER_OUTPUT)
             for rh in range(2):
-                place = ROWS_LOW * WINDOW * rh + PLACES * group
-                for a in range(0, HEADS_PER_CHUNK, HEADS_PER_STORE):
-                    nc.sync.dma_start(
-                        out=out[
-                            :, head + a : head + a + HEADS_PER_STORE, place : place + PLACES, :
-                        ],
-                        in_=o_tile[rh:P:2, a : a + HEADS_PER_STORE, :, :],
-                    )
+                place = GROUPS * WINDOW * rh + WINDOW * group
+                nc.sync.dma_start(
+                    out=out[:, head : head + HEADS_PER_CHUNK, place : place + WINDOW, :],
+                    in_=o_tile[rh:P:2, :, :, :],
+                )
 
-        measure(0)
-        measure_scalar(0)
-        measure(1)
-        measure_scalar(1)
-        centre_and_turn(0)
-        scale_out(0)
-        centre_and_turn(1)
-        scale_out(1)
-        measure(2)
-        measure_scalar(2)
-        pack(0)
-        nc.vector.tensor_copy(out=qkv_bias[:], in_=qkv_bias_bf[:])
-        quantise_weights(0)
-        pack(1)
-        for chunk in range(1, CHUNKS):
+        for i in (0, 1):
+            measure(i, FIRST_HALF)
+            measure(i, SECOND_HALF)
+            aggregate(i)
+            root(i)
+        for i in (0, 1):
+            invert(i)
+            centre(i, nc.vector)
+            turn(i)
+            scale_out(i, FIRST_HALF)
+            scale_out(i, SECOND_HALF)
+        measure(2, FIRST_HALF)
+        measure(2, SECOND_HALF)
+        aggregate(2)
+        root(2)
+        regroup(0, nc.vector.tensor_copy)
+        quantise(0)
+        invert(2)
+        centre(2, nc.gpsimd)
+        regroup(1, nc.vector.tensor_copy)
+        quantise(1)
+        for chunk in range(CHUNKS):
             quantise_weights(chunk)
-        centre_and_turn(2)
-        scale_out(2)
+        nc.vector.tensor_copy(out=qkv_bias[:], in_=qkv_bias_bf[:])
+        turn(2)
+        scale_out(2, FIRST_HALF)
+        measure(3, FIRST_HALF)
 
         for step in range(GROUPS * CHUNKS):
             group, chunk = divmod(step, CHUNKS)
-            i, ln_stage = 3 + step // LN_STAGES, step % LN_STAGES
+            i, phase = 3 + step // PERIOD, step % PERIOD
             banks = multiply(group, chunk)
-            if ln_stage == 0 and i < ROUNDS:
-                measure(i)
-            if ln_stage == 1 and i < ROUNDS:
-                centre(i)
-            if ln_stage == 2 and i < ROUNDS:
+            if phase == 0 and i < ROUNDS:
+                measure(i, SECOND_HALF)
+                aggregate(i)
+            if phase == 1 and i < ROUNDS:
+                invert(i)
+            if phase == 2 and i < ROUNDS:
                 turn(i)
-            if ln_stage == 2 and i - 1 < ROUNDS:
-                pack(i - 1)
-            store(group, chunk, banks)
-            if ln_stage == 0 and i < ROUNDS:
-                measure_scalar(i)
-            if ln_stage == 2 and i < ROUNDS:
-                scale_out(i)
+            if phase == 2 and i - 1 < ROUNDS:
+                quantise(i - 1)
+            if phase == 2 and i + 1 < ROUNDS:
+                measure(i + 1, FIRST_HALF)
+            store(group, chunk, banks, all_on_vector=(phase == 1))
+            if phase == 0 and i < ROUNDS:
+                root(i)
+            if phase == 0 and i - 1 < ROUNDS:
+                scale_out(i - 1, SECOND_HALF)
+            if phase == 1 and i < ROUNDS:
+                centre(i, nc.gpsimd)
+            if phase == 1 and i - 1 < ROUNDS:
+                regroup(i - 1, nc.scalar.copy)
+            if phase == 2 and i < ROUNDS:
+                scale_out(i, FIRST_HALF)

@@ -28,6 +28,7 @@ GROUPS = 4
 ROUND = 4
 ROUNDS = GROUPS * WINDOW // ROUND
 FIRST_HALF, SECOND_HALF = (0, 1), (2, 3)
+RUN = 4
 WEIGHT_TILES = OUT_CHANNELS // P
 
 CHUNK = 256
@@ -196,7 +197,10 @@ def tile_swintransformerblock_pa_t_kernel(
 
         def regroup(i, copy):
             words_of[i] = stage.tile([P, ROUND * P, PACK], BF16, name="h_words", align_bytes=64)
-            copy(out=words_of[i][:], in_=planes_of[i][:].rearrange("p t r -> p r t"))
+            copy(
+                out=words_of[i][:].rearrange("p (r e) t -> p r t e", e=RUN),
+                in_=planes_of[i][:].rearrange("p t (r e) -> p r t e", e=RUN),
+            )
 
         def quantise(i):
             columns = slice(ROUND * P * i, ROUND * P * (i + 1))
@@ -291,9 +295,12 @@ def tile_swintransformerblock_pa_t_kernel(
         centre(2, nc.gpsimd)
         regroup(1, nc.vector.tensor_copy)
         quantise(1)
+        nc.gpsimd.tensor_scalar(
+            out=qkv_bias[:], in0=qkv_bias_bf[:], scalar1=1.0, scalar2=0.0,
+            op0=ALU.mult, op1=ALU.add,
+        )
         for chunk in range(CHUNKS):
             quantise_weights(chunk)
-        nc.vector.tensor_copy(out=qkv_bias[:], in_=qkv_bias_bf[:])
         turn(2)
         scale_out(2, FIRST_HALF)
         measure(3, FIRST_HALF)

@@ -38,6 +38,7 @@ CHUNKS_PER_OUTPUT = CHANNELS // CHUNK
 TILES_PER_BANK = BANK // CHUNK
 BANKS_PER_CHUNK = WINDOW // TILES_PER_BANK
 PERIOD = CHUNKS * ROUND // WINDOW
+SCALAR_BANKS = (1, 0, 2)
 
 
 def rotate_columns(nc, out, in_, block, shift):
@@ -247,7 +248,7 @@ def tile_swintransformerblock_pa_t_kernel(
                 banks.append(acc)
             return banks
 
-        def store(group, chunk, banks, all_on_vector):
+        def store(group, chunk, banks, scalar_banks):
             bias = (
                 qkv_bias[:, CHUNK * chunk : CHUNK * (chunk + 1)]
                 .rearrange("p (a d) -> p a d", d=HEAD_DIM)
@@ -260,11 +261,11 @@ def tile_swintransformerblock_pa_t_kernel(
                     :, :, TILES_PER_BANK * bank : TILES_PER_BANK * (bank + 1), :
                 ].rearrange("p a c d -> p c a d")
                 src = acc[:].rearrange("p c (a d) -> p c a d", d=HEAD_DIM)
-                if all_on_vector or bank % 2 == 0:
-                    nc.vector.tensor_tensor(out=dst, in0=src, in1=bias, op=ALU.add)
-                else:
+                if bank % 2 == 1 and bank // 2 < scalar_banks:
                     nc.scalar.copy(out=dst, in_=src)
                     nc.gpsimd.tensor_tensor(out=dst, in0=dst, in1=bias, op=ALU.add)
+                else:
+                    nc.vector.tensor_tensor(out=dst, in0=src, in1=bias, op=ALU.add)
             out = outs[chunk // CHUNKS_PER_OUTPUT]
             head = HEADS_PER_CHUNK * (chunk % CHUNKS_PER_OUTPUT)
             for rh in range(2):
@@ -320,7 +321,7 @@ def tile_swintransformerblock_pa_t_kernel(
                 quantise(i - 1)
             if phase == 2 and i + 1 < ROUNDS:
                 measure(i + 1, FIRST_HALF)
-            store(group, chunk, banks, all_on_vector=(phase == 1))
+            store(group, chunk, banks, SCALAR_BANKS[phase])
             if phase == 0 and i < ROUNDS:
                 root(i)
             if phase == 0 and i - 1 < ROUNDS:

from contextlib import ExitStack

import concourse.mybir as mybir
from concourse.masks import make_identity

F32 = mybir.dt.float32
BF16 = mybir.dt.bfloat16
U32 = mybir.dt.uint32
U8 = mybir.dt.uint8
FP8X4 = mybir.dt.float8_e4m3fn_x4
ACT = mybir.ActivationFunctionType
ALU = mybir.AluOpType

P = 128
PACK = 4
BANK = 512
IMAGES, SIDE, CHANNELS = 4, 32, 512
WINDOW = 8
BLOCKS = SIDE // WINDOW
SHIFT = 3
HEADS, HEAD_DIM = 16, 32
EPS = 1e-5
TOKENS = IMAGES * SIDE * SIDE
OUT_CHANNELS = 3 * CHANNELS
FLOPS = 2 * TOKENS * CHANNELS * OUT_CHANNELS

GROUPS = 4
ROUND = 4
ROUNDS = GROUPS * WINDOW // ROUND
FIRST_HALF, SECOND_HALF = (0, 1), (2, 3)
RUN = 4
WEIGHT_TILES = OUT_CHANNELS // P

CHUNK = 256
CHUNKS = OUT_CHANNELS // CHUNK
HEADS_PER_CHUNK = CHUNK // HEAD_DIM
CHUNKS_PER_OUTPUT = CHANNELS // CHUNK
TILES_PER_BANK = BANK // CHUNK
BANKS_PER_CHUNK = WINDOW // TILES_PER_BANK
PERIOD = CHUNKS * ROUND // WINDOW
SCALAR_BANKS = (1, 0, 2)


def rotate_columns(nc, out, in_, block, shift):
    dst = out.rearrange("p (g c) -> p g c", c=block)
    src = in_.rearrange("p (g c) -> p g c", c=block)
    nc.vector.tensor_copy(out=dst[:, :, 0 : block - shift], in_=src[:, :, shift:block])
    nc.vector.tensor_copy(out=dst[:, :, block - shift : block], in_=src[:, :, 0:shift])


def tile_swintransformerblock_pa_t_kernel(
    tc, x, norm1_w, norm1_b, qkv_w, qkv_b, out_0, out_1, out_2
):
    nc = tc.nc
    outs = (out_0, out_1, out_2)

    with ExitStack() as ctx:
        const = ctx.enter_context(tc.tile_pool(name="const", bufs=1))
        small = ctx.enter_context(tc.tile_pool(name="small", bufs=4))
        z_pool = ctx.enter_context(tc.tile_pool(name="z", bufs=3))
        stage = ctx.enter_context(tc.tile_pool(name="stage", bufs=2))
        o_pool = ctx.enter_context(tc.tile_pool(name="o", bufs=CHUNKS))
        turned = ctx.enter_context(tc.psum_pool(name="turned", bufs=4))
        products = ctx.enter_context(tc.psum_pool(name="products", bufs=4))
        ctx.enter_context(tc.manual_schedule())

        x_view = x.rearrange(
            "b (iq il jb jc) k -> il jb (b iq) jc k", il=GROUPS, jb=BLOCKS, jc=WINDOW
        )
        x_tiles = [
            const.tile([P, WINDOW, CHANNELS], BF16, name="x_il%d" % il) for il in range(GROUPS)
        ]

        def load_round(i):
            il = (i * ROUND // WINDOW + SHIFT) % GROUPS
            columns = slice(i * ROUND % WINDOW, i * ROUND % WINDOW + ROUND)
            for jb in range(BLOCKS):
                nc.sync.dma_start(
                    out=x_tiles[il][jb:P:BLOCKS, columns, :], in_=x_view[il, jb][:, columns, :]
                )

        gain_bias_rows = const.tile([P, P], BF16)
        nc.vector.memset(gain_bias_rows[:], 0.0)
        nc.scalar.dma_start(
            out=gain_bias_rows[0:PACK, :], in_=norm1_w.rearrange("(t p) -> t p", p=P)
        )
        nc.scalar.dma_start(
            out=gain_bias_rows[PACK : 2 * PACK, :], in_=norm1_b.rearrange("(t p) -> t p", p=P)
        )

        w_raw = const.tile([P, WEIGHT_TILES, CHANNELS], BF16)
        qkv_bias_bf = const.tile([P, OUT_CHANNELS], BF16)
        for i in range(4):
            load_round(i)
        nc.sync.dma_start(out=w_raw[:], in_=qkv_w.rearrange("(f p) k -> p f k", p=P))
        nc.sync.dma_start(out=qkv_bias_bf[:], in_=qkv_b.partition_broadcast(P))
        for i in range(4, ROUNDS):
            load_round(i)

        ident_bf = const.tile([P, P], BF16)
        make_identity(nc, ident_bf[:])
        ident = const.tile([P, P], F32)
        make_identity(nc, ident[:])
        eps_col = const.tile([P, 1], F32)
        nc.vector.memset(eps_col[:], EPS)

        rolled = {(0, 0): ident}
        for rs, cs in ((0, 1), (1, 0), (1, 1)):
            rolled[(rs, cs)] = const.tile([P, P], F32, name="rolled%d%d" % (rs, cs))
        rotate_columns(nc, rolled[(0, 1)][:], ident[:], block=4, shift=1)
        rotate_columns(nc, rolled[(1, 0)][:], ident[:], block=32, shift=4)
        rotate_columns(nc, rolled[(1, 1)][:], rolled[(0, 1)][:], block=32, shift=4)
        perm = {}
        for key in rolled:
            perm[key] = const.tile([P, P], F32, name="perm%d%d" % key)
            nc.vector.tensor_copy(
                out=perm[key][:].rearrange("p (m wj rh) -> p m rh wj", wj=4, rh=2),
                in_=rolled[key][:].rearrange("p (m rh wj) -> p m rh wj", rh=2, wj=4),
            )

        gain_bias_t = turned.tile([P, P], BF16, tag="turned")
        nc.tensor.transpose(out=gain_bias_t[:], in_=gain_bias_rows[:], identity=ident_bf[:])
        gain_bias = const.tile([P, 2 * PACK], F32)
        nc.vector.tensor_copy(out=gain_bias[:], in_=gain_bias_t[:, 0 : 2 * PACK])

        qkv_bias = const.tile([P, OUT_CHANNELS], F32)

        x_codes = const.tile([P, TOKENS], U32, align_bytes=64)
        x_scales = const.tile([P, TOKENS], U8, align_bytes=64)
        w_codes = const.tile([P, OUT_CHANNELS], U32, align_bytes=64)
        w_scales = const.tile([P, OUT_CHANNELS], U8, align_bytes=64)

        stats_of, mean_var_of, std_of, rstd_of, offset_of = {}, {}, {}, {}, {}
        z_of, turned_of, planes_of, words_of = {}, {}, {}, {}

        def source(i, u):
            r_lo, jc = divmod(ROUND * i + u, WINDOW)
            key = (1 if r_lo > 0 else 0, 1 if jc < SHIFT else 0)
            return x_tiles[(r_lo + SHIFT) % GROUPS][:, jc, :], perm[key]

        def measure(i, tiles):
            if i not in stats_of:
                stats_of[i] = small.tile([P, ROUND, 6], F32, name="stats")
            for u in tiles:
                nc.vector.bn_stats(out=stats_of[i][:, u, :], in_=source(i, u)[0])

        def aggregate(i):
            mean_var_of[i] = small.tile([P, ROUND, 2], F32, name="mean_var")
            for u in range(ROUND):
                nc.vector.bn_aggr(out=mean_var_of[i][:, u, :], in_=stats_of[i][:, u, :])

        def root(i):
            std_of[i] = small.tile([P, ROUND], F32, name="std")
            nc.scalar.activation(
                out=std_of[i][:], in_=mean_var_of[i][:, :, 1], func=ACT.Sqrt, bias=eps_col[:],
                scale=1.0,
            )

        def invert(i):
            rstd_of[i] = small.tile([P, ROUND], F32, name="rstd")
            nc.vector.reciprocal(out=rstd_of[i][:], in_=std_of[i][:])
            offset_of[i] = small.tile([P, ROUND], F32, name="offset")
            nc.vector.scalar_tensor_tensor(
                out=offset_of[i][:], in0=mean_var_of[i][:, :, 0], scalar=-1.0, in1=rstd_of[i][:],
                op0=ALU.mult, op1=ALU.mult,
            )

        def centre(i, engine):
            z_of[i] = z_pool.tile([P, ROUND, CHANNELS], F32, name="z")
            for u in range(ROUND):
                engine.tensor_scalar(
                    out=z_of[i][:, u, :], in0=source(i, u)[0],
                    scalar1=rstd_of[i][:, u : u + 1], scalar2=offset_of[i][:, u : u + 1],
                    op0=ALU.mult, op1=ALU.add,
                )

        def turn(i):
            turned_of[i] = []
            for t in range(PACK):
                z_t = turned.tile([P, ROUND, P], F32, tag="turned")
                for u in range(ROUND):
                    nc.tensor.transpose(
                        out=z_t[:, u, :], in_=z_of[i][:, u, P * t : P * (t + 1)],
                        identity=source(i, u)[1][:],
                    )
                turned_of[i].append(z_t)

        def scale_out(i, planes):
            if i not in planes_of:
                planes_of[i] = stage.tile([P, PACK, ROUND * P], BF16, name="h_planes")
            for t in planes:
                nc.scalar.activation(
                    out=planes_of[i][:, t, :],
                    in_=turned_of[i][t][:].rearrange("p u r -> p (u r)"),
                    func=ACT.Identity,
                    scale=gain_bias[:, t : t + 1], bias=gain_bias[:, PACK + t : PACK + t + 1],
                )

        def regroup(i, copy):
            words_of[i] = stage.tile([P, ROUND * P, PACK], BF16, name="h_words", align_bytes=64)
            copy(
                out=words_of[i][:].rearrange("p (r e) t -> p r t e", e=RUN),
                in_=planes_of[i][:].rearrange("p t (r e) -> p r t e", e=RUN),
            )

        def quantise(i):
            columns = slice(ROUND * P * i, ROUND * P * (i + 1))
            nc.vector.quantize_mx(
                out=x_codes[:, columns].bitcast(FP8X4),
                scales=x_scales[:, columns],
                in_=words_of[i][:].rearrange("p r t -> p (r t)"),
            )

        def quantise_weights(chunk):
            tiles = CHUNK // P
            w_t = turned.tile([P, tiles, PACK, P], BF16, tag="turned")
            for f in range(tiles):
                for t in range(PACK):
                    nc.tensor.transpose(
                        out=w_t[:, f, t, :], in_=w_raw[:, tiles * chunk + f, P * t : P * (t + 1)],
                        identity=ident_bf[:],
                    )
            w_words = stage.tile([P, tiles, P, PACK], BF16, align_bytes=64)
            nc.scalar.copy(out=w_words[:], in_=w_t[:].rearrange("p f t c -> p f c t"))
            nc.vector.quantize_mx(
                out=w_codes[:, CHUNK * chunk : CHUNK * (chunk + 1)].bitcast(FP8X4),
                scales=w_scales[:, CHUNK * chunk : CHUNK * (chunk + 1)],
                in_=w_words[:].rearrange("p f c t -> p (f c t)"),
            )

        def multiply(group, chunk):
            channels = slice(CHUNK * chunk, CHUNK * (chunk + 1))
            banks = []
            for bank in range(BANKS_PER_CHUNK):
                acc = products.tile([P, TILES_PER_BANK, CHUNK], F32)
                for u in range(TILES_PER_BANK):
                    c = TILES_PER_BANK * bank + u
                    first = P * (WINDOW * group + (c + SHIFT) % WINDOW)
                    nc.tensor.matmul_mx(
                        out=acc[:, u, :],
                        lhsT=x_codes[:, first : first + P].bitcast(FP8X4),
                        lhsT_scale=x_scales[:, first : first + P],
                        rhs=w_codes[:, channels].bitcast(FP8X4),
                        rhs_scale=w_scales[:, channels],
                        start=True,
                        stop=True,
                    )
                banks.append(acc)
            return banks

        def store(group, chunk, banks, scalar_banks):
            bias = (
                qkv_bias[:, CHUNK * chunk : CHUNK * (chunk + 1)]
                .rearrange("p (a d) -> p a d", d=HEAD_DIM)
                .unsqueeze(1)
                .to_broadcast([P, TILES_PER_BANK, HEADS_PER_CHUNK, HEAD_DIM])
            )
            o_tile = o_pool.tile([P, HEADS_PER_CHUNK, WINDOW, HEAD_DIM], F32)
            for bank, acc in enumerate(banks):
                dst = o_tile[
                    :, :, TILES_PER_BANK * bank : TILES_PER_BANK * (bank + 1), :
                ].rearrange("p a c d -> p c a d")
                src = acc[:].rearrange("p c (a d) -> p c a d", d=HEAD_DIM)
                if bank % 2 == 1 and bank // 2 < scalar_banks:
                    nc.scalar.copy(out=dst, in_=src)
                    nc.gpsimd.tensor_tensor(out=dst, in0=dst, in1=bias, op=ALU.add)
                else:
                    nc.vector.tensor_tensor(out=dst, in0=src, in1=bias, op=ALU.add)
            out = outs[chunk // CHUNKS_PER_OUTPUT]
            head = HEADS_PER_CHUNK * (chunk % CHUNKS_PER_OUTPUT)
            for rh in range(2):
                place = GROUPS * WINDOW * rh + WINDOW * group
                nc.sync.dma_start(
                    out=out[:, head : head + HEADS_PER_CHUNK, place : place + WINDOW, :],
                    in_=o_tile[rh:P:2, :, :, :],
                )

        for i in (0, 1):
            measure(i, FIRST_HALF)
            measure(i, SECOND_HALF)
            aggregate(i)
            root(i)
        for i in (0, 1):
            invert(i)
            centre(i, nc.vector)
            turn(i)
            scale_out(i, FIRST_HALF)
            scale_out(i, SECOND_HALF)
        measure(2, FIRST_HALF)
        measure(2, SECOND_HALF)
        aggregate(2)
        root(2)
        regroup(0, nc.vector.tensor_copy)
        quantise(0)
        invert(2)
        centre(2, nc.gpsimd)
        regroup(1, nc.vector.tensor_copy)
        quantise(1)
        nc.gpsimd.tensor_scalar(
            out=qkv_bias[:], in0=qkv_bias_bf[:], scalar1=1.0, scalar2=0.0,
            op0=ALU.mult, op1=ALU.add,
        )
        for chunk in range(CHUNKS):
            quantise_weights(chunk)
        turn(2)
        scale_out(2, FIRST_HALF)
        measure(3, FIRST_HALF)

        for step in range(GROUPS * CHUNKS):
            group, chunk = divmod(step, CHUNKS)
            i, phase = 3 + step // PERIOD, step % PERIOD
            banks = multiply(group, chunk)
            if phase == 0 and i < ROUNDS:
                measure(i, SECOND_HALF)
                aggregate(i)
            if phase == 1 and i < ROUNDS:
                invert(i)
            if phase == 2 and i < ROUNDS:
                turn(i)
            if phase == 2 and i - 1 < ROUNDS:
                quantise(i - 1)
            if phase == 2 and i + 1 < ROUNDS:
                measure(i + 1, FIRST_HALF)
            store(group, chunk, banks, SCALAR_BANKS[phase])
            if phase == 0 and i < ROUNDS:
                root(i)
            if phase == 0 and i - 1 < ROUNDS:
                scale_out(i - 1, SECOND_HALF)
            if phase == 1 and i < ROUNDS:
                centre(i, nc.gpsimd)
            if phase == 1 and i - 1 < ROUNDS:
                regroup(i - 1, nc.scalar.copy)
            if phase == 2 and i < ROUNDS:
                scale_out(i, FIRST_HALF)
